import numpy as np
import ml_dtypes


def mxq(x, axis, fmt="e4m3"):
    dtype, down = {"e4m3": (ml_dtypes.float8_e4m3fn, 7), "e5m2": (ml_dtypes.float8_e5m2, 14)}[fmt]
    v = np.moveaxis(np.asarray(x, np.float32).astype(ml_dtypes.bfloat16).astype(np.float64), axis, -1)
    blocks = v.reshape(v.shape[:-1] + (-1, 32))
    amax = np.abs(blocks).max(-1, keepdims=True)
    byte = np.maximum(np.where(amax > 0, np.frexp(amax)[1] - 1 + 127, 0) - down, 1)
    scale = np.exp2(byte - 127.0)
    codes = (blocks / scale).astype(np.float32).astype(dtype).astype(np.float64)
    return np.moveaxis((codes * scale).reshape(v.shape), -1, axis)


WIDE = False


def mx_kscale(k):
    if not WIDE:
        return np.ones(k)
    levels = np.array([10, -10, 5, -5, 0])
    if k % 512:
        return np.exp2(np.random.permutation(np.resize(levels, k // 32))).repeat(32)
    a = np.empty((k // 512, 16))
    for p in range(k // 512):
        a[p, :8] = np.random.permutation(np.resize(levels, 8))
        for g in range(8):
            far = levels[np.abs(levels - a[p, g]) >= 10]
            a[p, g + 8] = far[np.random.randint(len(far))]
    return np.exp2(a.ravel()).repeat(32)


BF16 = ml_dtypes.bfloat16


def bf(x):
    return np.asarray(x, np.float32).astype(BF16)


def f64(x):
    return np.asarray(x).astype(np.float64)


B, S, D, H, NOPE, ROPE, VD, KV_RANK, Q_RANK = 2, 1024, 4096, 16, 128, 128, 128, 512, 3072
EPS = 1e-6
THETA = 10000.0
LAT = 0.005
HALF = ROPE // 2
QK = NOPE + ROPE


def rmsnorm(v, g):
    return v * (1.0 / np.sqrt(np.mean(v * v, axis=-1, keepdims=True) + EPS)) * g


def rope(v):
    inv = 1.0 / THETA ** (np.arange(HALF) / HALF)
    ang = np.arange(S)[:, None] * inv[None, :]
    cos = np.cos(ang)[None, :, None, :]
    sin = np.sin(ang)[None, :, None, :]
    v1, v2 = v[..., :HALF], v[..., HALF:]
    return np.concatenate([v1 * cos - v2 * sin, v2 * cos + v1 * sin], axis=-1)


def setup_inputs():
    s, t = mx_kscale(D), mx_kscale(Q_RANK)
    return {"x": bf(np.random.standard_normal((B, S, D)) * s),
            "w_dq": bf(np.random.standard_normal((D, Q_RANK)) * LAT / np.sqrt(D) / s[:, None]),
            "q_a_norm": bf((1.0 + 0.1 * np.random.standard_normal(Q_RANK)) * t),
            "w_uq": bf(np.random.standard_normal((Q_RANK, H * QK)) / np.sqrt(Q_RANK) / t[:, None])}


def reference(x, w_dq, q_a_norm, w_uq):
    c_q = mxq(f64(x), 2, "e4m3") @ mxq(f64(w_dq), 0, "e4m3")
    h = rmsnorm(c_q, f64(q_a_norm))
    q = (mxq(h, 2, "e4m3") @ mxq(f64(w_uq), 0, "e4m3")).reshape(B, S, H, QK)
    q_nope, q_pe = q[..., :NOPE], q[..., NOPE:]
    return np.concatenate([q_nope, rope(q_pe)], axis=-1)

@@ -1,0 +1,413 @@
+from contextlib import ExitStack
+
+import concourse.mybir as mybir
+from concourse.masks import make_identity
+
+F32 = mybir.dt.float32
+BF16 = mybir.dt.bfloat16
+U32 = mybir.dt.uint32
+U8 = mybir.dt.uint8
+I32 = mybir.dt.int32
+FP8X4 = mybir.dt.float8_e4m3fn_x4
+ALU = mybir.AluOpType
+ACT = mybir.ActivationFunctionType
+AX = mybir.AxisListType
+
+P = 128
+TOK = 2048
+NB = TOK // P
+D = 4096
+G1 = D // 512
+R = 3072
+C1 = R // 512
+FO = 4096
+C2 = FO // 512
+PARK = 4
+EPS = 1e-6
+TWO_PI = 6.283185307179586
+FLOPS = 2 * TOK * D * R + 2 * TOK * R * FO
+
+WSLOTS = 24
+
+
+def tile_multiheadlatentattention_pa_l_kernel(tc, x, w_dq, q_a_norm, w_uq, out):
+    nc = tc.nc
+    x2 = x.rearrange("b s d -> (b s) d")
+    o2 = out.rearrange("b s h f -> (b s) (h f)")
+
+    wlist = [(0, n, g) for n in range(C1) for g in range(G1)] + [(1, m, g) for m in range(C2) for g in range(C1)]
+    NW = len(wlist)
+    raw = {}
+    grp = {}
+    codes = {}
+    xraw = {}
+    xgrp = {}
+    xcod = {}
+    hcod = {}
+    accs = {}
+    crs = {}
+    rrs = {}
+    hbs = {}
+
+    with ExitStack() as ctx:
+        keep = ctx.enter_context(tc.tile_pool(name="keep", bufs=1))
+        xp = ctx.enter_context(tc.tile_pool(name="xp", bufs=NB))
+        wp = ctx.enter_context(tc.tile_pool(name="wp", bufs=4))
+        sp = ctx.enter_context(tc.tile_pool(name="sp", bufs=4))
+        sm = ctx.enter_context(tc.tile_pool(name="sm", bufs=3))
+        ps = ctx.enter_context(tc.psum_pool(name="ps", bufs=8))
+
+        ident = keep.tile([P, P], F32, name="ident")
+        make_identity(nc, ident[:])
+        neghalf = keep.tile([P, 1], F32, name="neghalf")
+        nc.vector.memset(neghalf[:], -0.5)
+        ss = keep.tile([P, NB, 8], F32, name="ss")
+        tab = keep.tile([P, 8, 128], F32, name="tab")
+
+        def w_load(q):
+            if q >= NW:
+                return
+            kind, n, g = wlist[q]
+            src = w_dq if kind == 0 else w_uq
+            t = wp.tile([P, 4, 512], BF16, name="wraw", tag="wraw", bufs=4)
+            nc.sync.dma_start(
+                out=t[:],
+                in_=src[512 * g : 512 * (g + 1), 512 * n : 512 * (n + 1)].rearrange("(p j) c -> p j c", j=4),
+            )
+            raw[q] = t
+
+        def w_ilv(q, eng):
+            t = wp.tile([P, 2048], BF16, name="wgrp", tag="wgrp", bufs=3, align_bytes=64)
+            o = t[:].rearrange("p (c j) -> p c j", j=4)
+            i = raw.pop(q)[:].rearrange("p j c -> p c j")
+            if eng == 0:
+                nc.vector.tensor_copy(out=o, in_=i)
+            else:
+                nc.scalar.copy(out=o, in_=i)
+            grp[q] = t
+
+        def w_qnt(q):
+            c = wp.tile([P, 512], U32, name="wc", tag="wc", bufs=WSLOTS, align_bytes=64)
+            s = wp.tile([P, 512], U8, name="ws", tag="ws", bufs=WSLOTS, align_bytes=64)
+            nc.vector.quantize_mx(out=c[:].bitcast(FP8X4), scales=s[:], in_=grp.pop(q)[:])
+            codes[q] = (c, s)
+
+        tick_state = [8, 8]
+
+        def tick(eng):
+            q = tick_state[0]
+            if q < NW:
+                w_ilv(q, eng)
+                w_load(q + 4)
+                tick_state[0] = q + 1
+            while tick_state[1] < tick_state[0] - (1 if tick_state[0] < NW else 0):
+                w_qnt(tick_state[1])
+                tick_state[1] = tick_state[1] + 1
+
+        def flush():
+            while tick_state[1] < tick_state[0]:
+                w_qnt(tick_state[1])
+                tick_state[1] = tick_state[1] + 1
+
+        def passes(acc, lc, ls, glist, qbase, ng):
+            for g in glist:
+                c, s = codes[qbase + g]
+                nc.tensor.matmul_mx(
+                    out=acc[:],
+                    lhsT=lc[:, 128 * g : 128 * (g + 1)].bitcast(FP8X4),
+                    lhsT_scale=ls[:, 128 * g : 128 * (g + 1)],
+                    rhs=c[:].bitcast(FP8X4),
+                    rhs_scale=s[:],
+                    start=(g == 0),
+                    stop=(g == ng - 1),
+                )
+
+        def bank():
+            b = ps.tile([P, 512], F32, name="bank", tag="bank", bufs=8)
+            return b
+
+        with tc.tile_pool(name="s1", bufs=1) as s1:
+            gain = s1.tile([P, R], BF16, name="gain")
+
+            def sorted_view(ap):
+                return ap.rearrange("q (p u e) -> q u p e", u=2, e=2)
+
+            def square(acc, i, n):
+                jk = s1.tile([P, 512], BF16, name="junk", tag="junk", bufs=2)
+                nc.scalar.activation(out=jk[:], in_=acc[:], func=ACT.Square, accum_out=ss[:, i, n : n + 1])
+
+            def evac_a(n, i):
+                acc = accs.pop((n, i))
+                square(acc, i, n)
+                st = sp.tile([P, 512], F32, name="st", tag="st", bufs=4)
+                nc.vector.tensor_tensor(
+                    out=st[:].rearrange("q (u p e) -> q u p e", u=2, e=2),
+                    in0=sorted_view(acc[:]),
+                    in1=sorted_view(gain[:, 512 * n : 512 * (n + 1)]),
+                    op=ALU.mult,
+                )
+                nc.sync.dma_start(out=o2[128 * i : 128 * (i + 1), 512 * n : 512 * (n + 1)], in_=st[:])
+
+            def p1a(n, i):
+                acc = bank()
+                lc, ls = xcod[i]
+                passes(acc, lc, ls, range(G1), G1 * n, G1)
+                accs[(n, i)] = acc
+
+            with tc.tile_pool(name="hp", bufs=2) as hp:
+
+                def x_load(i):
+                    if i >= NB:
+                        return
+                    t = hp.tile([P, D], BF16, name="xraw", tag="xraw", bufs=2)
+                    nc.sync.dma_start(out=t[:], in_=x2[128 * i : 128 * (i + 1), :])
+                    xraw[i] = t
+
+                def x_tr(i, engs):
+                    xw = xraw.pop(i)[:].bitcast(F32)
+                    xg = hp.tile([P, D], BF16, name="xgrp", tag="xgrp", bufs=2, align_bytes=64)
+                    xgw = xg[:].bitcast(F32)
+                    for b in range(4):
+                        bk = bank()
+                        for jj in range(4):
+                            g = 2 * b + jj // 2
+                            u = jj % 2
+                            nc.tensor.transpose(
+                                out=bk[:, 128 * jj : 128 * (jj + 1)],
+                                in_=xw[:, 256 * g + u : 256 * (g + 1) : 2],
+                                identity=ident[:],
+                            )
+                        o = xgw[:, 512 * b : 512 * (b + 1)].rearrange("p (g r u) -> p g r u", g=2, u=2)
+                        i_ = bk[:].rearrange("p (g u r) -> p g r u", g=2, u=2)
+                        if engs[b] == 0:
+                            nc.vector.tensor_copy(out=o, in_=i_)
+                        else:
+                            nc.scalar.copy(out=o, in_=i_)
+                    xgrp[i] = xg
+
+                def x_qnt(i):
+                    c = xp.tile([P, 1024], U32, name="xc", tag="xc", bufs=NB, align_bytes=64)
+                    s = xp.tile([P, 1024], U8, name="xs", tag="xs", bufs=NB, align_bytes=64)
+                    nc.vector.quantize_mx(out=c[:].bitcast(FP8X4), scales=s[:], in_=xgrp.pop(i)[:])
+                    xcod[i] = (c, s)
+
+                x_load(0)
+                w_load(0)
+                w_load(1)
+                x_load(1)
+                w_load(2)
+                w_load(3)
+                for k in range(4):
+                    x_tr(k, (0, 1, 0, 1))
+                    x_load(k + 2)
+                    w_ilv(2 * k, 0)
+                    w_ilv(2 * k + 1, 1)
+                    w_load(2 * k + 4)
+                    w_load(2 * k + 5)
+                    if k == 2:
+                        nc.sync.dma_start(out=gain[:], in_=q_a_norm.partition_broadcast(P))
+                    x_qnt(k)
+                    w_qnt(2 * k)
+                    w_qnt(2 * k + 1)
+                    accs[(0, k)] = bank()
+                    lc, ls = xcod[k]
+                    passes(accs[(0, k)], lc, ls, range(2 * k), 0, G1)
+                    for kk in range(k + 1):
+                        lc, ls = xcod[kk]
+                        passes(accs[(0, kk)], lc, ls, (2 * k, 2 * k + 1), 0, G1)
+                x_tr(4, (0, 1, 0, 1))
+                x_load(6)
+                x_qnt(4)
+                for k in range(4):
+                    evac_a(0, k)
+                for i in range(4, NB):
+                    p1a(0, i)
+                    if i + 1 < NB:
+                        x_tr(i + 1, (0, 0, 0, 1))
+                        x_load(i + 3)
+                    if i > 4:
+                        evac_a(0, i - 1)
+                    if i + 1 < NB:
+                        x_qnt(i + 1)
+                    if i % 3 != 0:
+                        tick(1)
+                evac_a(0, NB - 1)
+                flush()
+
+            with tc.tile_pool(name="tb", bufs=1) as tb:
+                posi = tb.tile([P, 8], I32, name="posi")
+                nc.gpsimd.iota(posi[:], pattern=[[128, 8]], base=0, channel_multiplier=1)
+                posf = tb.tile([P, 8], F32, name="posf")
+                nc.vector.tensor_copy(out=posf[:], in_=posi[:])
+                turns = tb.tile([P, 8, 128], F32, name="turns")
+                whole_i = tb.tile([P, 8, 128], I32, name="whole_i")
+                whole_f = tb.tile([P, 8, 128], F32, name="whole_f")
+
+                def tab_column(f):
+                    inv = (10000.0 ** (-f / 64.0)) / TWO_PI
+                    nc.gpsimd.tensor_scalar(
+                        out=turns[:, :, f], in0=posf[:], scalar1=inv, scalar2=0.0, op0=ALU.mult, op1=ALU.add
+                    )
+                    nc.gpsimd.tensor_scalar(
+                        out=turns[:, :, 64 + f], in0=posf[:], scalar1=inv, scalar2=0.25, op0=ALU.mult, op1=ALU.add
+                    )
+
+                for i in range(NB):
+                    p1a(1, i)
+                    if i > 0:
+                        evac_a(1, i - 1)
+                    if i % 4 != 3:
+                        tick(i % 2)
+                    for f in range(4 * i, 4 * i + 4):
+                        tab_column(f)
+                evac_a(1, NB - 1)
+                nc.vector.tensor_copy(out=whole_i[:], in_=turns[:])
+                nc.vector.tensor_copy(out=whole_f[:], in_=whole_i[:])
+                nc.vector.tensor_tensor(out=turns[:], in0=turns[:], in1=whole_f[:], op=ALU.subtract)
+                nc.vector.scalar_tensor_tensor(
+                    out=whole_f[:].rearrange("p b f -> p (b f)"),
+                    in0=turns[:].rearrange("p b f -> p (b f)"),
+                    scalar=0.5,
+                    in1=turns[:].rearrange("p b f -> p (b f)"),
+                    op0=ALU.is_gt,
+                    op1=ALU.subtract,
+                )
+                nc.scalar.activation(out=tab[:], in_=whole_f[:], func=ACT.Sin, scale=-TWO_PI)
+
+            with tc.tile_pool(name="bp", bufs=2) as bp:
+
+                def cr_load(i):
+                    if i >= NB:
+                        return
+                    t = bp.tile([P, 512 * PARK], F32, name="cr", tag="cr", bufs=2)
+                    nc.sync.dma_start(out=t[:], in_=o2[128 * i : 128 * (i + 1), 0 : 512 * PARK])
+                    crs[i] = t
+
+                def p1b(i):
+                    lc, ls = xcod.pop(i)
+                    for n in (PARK, PARK + 1):
+                        acc = bank()
+                        passes(acc, lc, ls, range(G1), G1 * n, G1)
+                        accs[(n, i)] = acc
+
+                def hmake(i):
+                    a4 = accs.pop((PARK, i))
+                    a5 = accs.pop((PARK + 1, i))
+                    square(a4, i, PARK)
+                    square(a5, i, PARK + 1)
+                    ssum = sm.tile([P, 1], F32, name="ssum", tag="ssum", bufs=3)
+                    nc.vector.tensor_reduce(out=ssum[:], in_=ss[:, i, 0:C1], axis=AX.X, op=ALU.add)
+                    ms = sm.tile([P, 1], F32, name="ms", tag="ms", bufs=3)
+                    nc.vector.tensor_scalar(
+                        out=ms[:], in0=ssum[:], scalar1=1.0 / R, scalar2=EPS, op0=ALU.mult, op1=ALU.add
+                    )
+                    rr = sm.tile([P, 1], F32, name="rr", tag="rr", bufs=3)
+                    nc.gpsimd.tensor_tensor(out=rr[:], in0=ms[:], in1=neghalf[:], op=ALU.pow)
+                    hb = bp.tile([P, R], BF16, name="hb", tag="hb", bufs=2, align_bytes=64)
+                    cr = crs.pop(i)
+                    for k, acc in enumerate((a4, a5)):
+                        n = PARK + k
+                        for u in range(2):
+                            lo = 512 * n + 256 * u
+                            nc.vector.scalar_tensor_tensor(
+                                out=hb[:, lo : lo + 256].rearrange("q (p e) -> q p e", e=2),
+                                in0=sorted_view(acc[:])[:, u],
+                                scalar=rr[:],
+                                in1=sorted_view(gain[:, 512 * n : 512 * (n + 1)])[:, u],
+                                op0=ALU.mult,
+                                op1=ALU.mult,
+                            )
+                    nc.scalar.activation(out=hb[:, 1024:2048], in_=cr[:, 1024:2048], func=ACT.Copy, scale=rr[:])
+                    nc.vector.tensor_scalar(
+                        out=hb[:, 0:1024], in0=cr[:, 0:1024], scalar1=rr[:], scalar2=None, op0=ALU.mult
+                    )
+                    hbs[i] = hb
+
+                def hfin(i):
+                    hw = hbs.pop(i)[:].bitcast(F32)
+                    hg = bp.tile([P, R], BF16, name="hg", tag="hg", bufs=1, align_bytes=64)
+                    hgw = hg[:].bitcast(F32)
+                    for b in range(3):
+                        bk = bank()
+                        for jj in range(4):
+                            j = 4 * b + jj
+                            nc.tensor.transpose(
+                                out=bk[:, 128 * jj : 128 * (jj + 1)],
+                                in_=hw[:, 128 * j : 128 * (j + 1)],
+                                identity=ident[:],
+                            )
+                        nc.scalar.copy(
+                            out=hgw[:, 512 * b : 512 * (b + 1)].rearrange("p (g r u) -> p g r u", g=2, u=2),
+                            in_=bk[:].rearrange("p (g u r) -> p g r u", g=2, u=2),
+                        )
+                    c = xp.tile([P, 768], U32, name="hc", tag="xc", bufs=NB, align_bytes=64)
+                    s = xp.tile([P, 768], U8, name="hs", tag="xs", bufs=NB, align_bytes=64)
+                    nc.vector.quantize_mx(out=c[:, 0:512].bitcast(FP8X4), scales=s[:, 0:512], in_=hg[:, 0:2048])
+                    nc.vector.quantize_mx(out=c[:, 512:768].bitcast(FP8X4), scales=s[:, 512:768], in_=hg[:, 2048:3072])
+                    hcod[i] = (c, s)
+
+                def p2(m, i):
+                    acc = bank()
+                    lc, ls = hcod[i]
+                    passes(acc, lc, ls, range(C1), G1 * C1 + C1 * m, C1)
+                    accs[(m, i)] = acc
+
+                def evac2(m, i):
+                    acc = accs.pop((m, i))
+                    av = acc[:].rearrange("q (h f) -> q h f", h=2)
+                    st = sp.tile([P, 512], F32, name="st", tag="st", bufs=4)
+                    sv = st[:].rearrange("q (h f) -> q h f", h=2)
+                    b = i % 8
+                    cosb = tab[:, b, 64:128].unsqueeze(1).unsqueeze(1).to_broadcast([P, 2, 2, 64])
+                    sinb = tab[:, b, 0:64].unsqueeze(1).unsqueeze(1).to_broadcast([P, 2, 2, 64])
+                    rot = av[:, :, 128:256].rearrange("q h (s f) -> q h s f", s=2)
+                    ra = sp.tile([P, 2, 2, 64], F32, name="ra", tag="ra", bufs=2)
+                    rb = sp.tile([P, 2, 2, 64], F32, name="rb", tag="rb", bufs=2)
+                    nc.vector.tensor_tensor(out=ra[:], in0=rot, in1=cosb, op=ALU.mult)
+                    nc.vector.tensor_tensor(out=rb[:], in0=rot, in1=sinb, op=ALU.mult)
+                    nc.scalar.copy(out=sv[:, :, 0:128], in_=av[:, :, 0:128])
+                    nc.vector.tensor_tensor(out=sv[:, :, 128:192], in0=ra[:, :, 0, :], in1=rb[:, :, 1, :], op=ALU.subtract)
+                    nc.vector.tensor_tensor(out=sv[:, :, 192:256], in0=ra[:, :, 1, :], in1=rb[:, :, 0, :], op=ALU.add)
+                    nc.sync.dma_start(out=o2[128 * i : 128 * (i + 1), 512 * m : 512 * (m + 1)], in_=st[:])
+
+                for n in (2, 3):
+                    for i in range(NB):
+                        p1a(n, i)
+                        if i > 0:
+                            evac_a(n, i - 1)
+                        if n == 2:
+                            if i % 4 != 3:
+                                tick(i % 2)
+                        elif i < 8:
+                            tick(i % 2)
+                        elif i == 8:
+                            flush()
+                        if n == 3 and i == 6:
+                            cr_load(0)
+                        if n == 3 and i == 12:
+                            cr_load(1)
+                    evac_a(n, NB - 1)
+
+                s2 = [(m, i) for m in range(C2) for i in range(NB)]
+                for i in range(NB + 2):
+                    if i < NB:
+                        p1b(i)
+                    else:
+                        p2(s2[i - NB][0], s2[i - NB][1])
+                    if i >= 2:
+                        hfin(i - 2)
+                    if 1 <= i <= NB:
+                        hmake(i - 1)
+                        cr_load(i + 1)
+                    if i == NB + 1:
+                        evac2(s2[0][0], s2[0][1])
+                    if i % 2 == 0 and i < NB:
+                        tick(0)
+
+        done = 2
+        for k in range(done, len(s2)):
+            p2(s2[k][0], s2[k][1])
+            evac2(s2[k - 1][0], s2[k - 1][1])
+            if (k * 9) % 20 < 9:
+                tick(1)
+        evac2(s2[-1][0], s2[-1][1])

@@ -42,6 +42,7 @@ def tile_multiheadlatentattention_pa_l_kernel(tc, x, w_dq, q_a_norm, w_uq, out):
     codes = {}
     xraw = {}
     xgrp = {}
+    xbank = {}
     xcod = {}
     hcod = {}
     accs = {}
@@ -56,6 +57,7 @@ def tile_multiheadlatentattention_pa_l_kernel(tc, x, w_dq, q_a_norm, w_uq, out):
         sp = ctx.enter_context(tc.tile_pool(name="sp", bufs=4))
         sm = ctx.enter_context(tc.tile_pool(name="sm", bufs=3))
         ps = ctx.enter_context(tc.psum_pool(name="ps", bufs=8))
+        ctx.enter_context(tc.manual_schedule())
 
         ident = keep.tile([P, P], F32, name="ident")
         make_identity(nc, ident[:])
@@ -163,10 +165,11 @@ def tile_multiheadlatentattention_pa_l_kernel(tc, x, w_dq, q_a_norm, w_uq, out):
                     nc.sync.dma_start(out=t[:], in_=x2[128 * i : 128 * (i + 1), :])
                     xraw[i] = t
 
-                def x_tr(i, engs):
+                def x_tr(i):
+                    if i >= NB:
+                        return
                     xw = xraw.pop(i)[:].bitcast(F32)
-                    xg = hp.tile([P, D], BF16, name="xgrp", tag="xgrp", bufs=2, align_bytes=64)
-                    xgw = xg[:].bitcast(F32)
+                    bks = []
                     for b in range(4):
                         bk = bank()
                         for jj in range(4):
@@ -177,8 +180,19 @@ def tile_multiheadlatentattention_pa_l_kernel(tc, x, w_dq, q_a_norm, w_uq, out):
                                 in_=xw[:, 256 * g + u : 256 * (g + 1) : 2],
                                 identity=ident[:],
                             )
+                        bks.append(bk)
+                    xbank[i] = bks
+                    x_load(i + 2)
+
+                def x_out(i, engs):
+                    if i >= NB:
+                        return
+                    xg = hp.tile([P, D], BF16, name="xgrp", tag="xgrp", bufs=2, align_bytes=64)
+                    xgw = xg[:].bitcast(F32)
+                    bks = xbank.pop(i)
+                    for b in range(4):
                         o = xgw[:, 512 * b : 512 * (b + 1)].rearrange("p (g r u) -> p g r u", g=2, u=2)
-                        i_ = bk[:].rearrange("p (g u r) -> p g r u", g=2, u=2)
+                        i_ = bks[b][:].rearrange("p (g u r) -> p g r u", g=2, u=2)
                         if engs[b] == 0:
                             nc.vector.tensor_copy(out=o, in_=i_)
                         else:
@@ -186,6 +200,8 @@ def tile_multiheadlatentattention_pa_l_kernel(tc, x, w_dq, q_a_norm, w_uq, out):
                     xgrp[i] = xg
 
                 def x_qnt(i):
+                    if i >= NB:
+                        return
                     c = xp.tile([P, 1024], U32, name="xc", tag="xc", bufs=NB, align_bytes=64)
                     s = xp.tile([P, 1024], U8, name="xs", tag="xs", bufs=NB, align_bytes=64)
                     nc.vector.quantize_mx(out=c[:].bitcast(FP8X4), scales=s[:], in_=xgrp.pop(i)[:])
@@ -197,9 +213,9 @@ def tile_multiheadlatentattention_pa_l_kernel(tc, x, w_dq, q_a_norm, w_uq, out):
                 x_load(1)
                 w_load(2)
                 w_load(3)
+                x_tr(0)
                 for k in range(4):
-                    x_tr(k, (0, 1, 0, 1))
-                    x_load(k + 2)
+                    x_out(k, (0, 1, 0, 1))
                     w_ilv(2 * k, 0)
                     w_ilv(2 * k + 1, 1)
                     w_load(2 * k + 4)
@@ -212,26 +228,23 @@ def tile_multiheadlatentattention_pa_l_kernel(tc, x, w_dq, q_a_norm, w_uq, out):
                     accs[(0, k)] = bank()
                     lc, ls = xcod[k]
                     passes(accs[(0, k)], lc, ls, range(2 * k), 0, G1)
+                    x_tr(k + 1)
                     for kk in range(k + 1):
                         lc, ls = xcod[kk]
                         passes(accs[(0, kk)], lc, ls, (2 * k, 2 * k + 1), 0, G1)
-                x_tr(4, (0, 1, 0, 1))
-                x_load(6)
+                x_out(4, (0, 1, 0, 1))
+                x_tr(5)
                 x_qnt(4)
-                for k in range(4):
-                    evac_a(0, k)
                 for i in range(4, NB):
                     p1a(0, i)
-                    if i + 1 < NB:
-                        x_tr(i + 1, (0, 0, 0, 1))
-                        x_load(i + 3)
-                    if i > 4:
-                        evac_a(0, i - 1)
-                    if i + 1 < NB:
-                        x_qnt(i + 1)
+                    x_out(i + 1, (0, 1, 0, 1))
+                    x_tr(i + 2)
+                    evac_a(0, i - 4)
+                    x_qnt(i + 1)
                     if i % 3 != 0:
                         tick(1)
-                evac_a(0, NB - 1)
+                for i in range(NB - 4, NB - 1):
+                    evac_a(0, i)
                 flush()
 
             with tc.tile_pool(name="tb", bufs=1) as tb:
@@ -252,27 +265,37 @@ def tile_multiheadlatentattention_pa_l_kernel(tc, x, w_dq, q_a_norm, w_uq, out):
                         out=turns[:, :, 64 + f], in0=posf[:], scalar1=inv, scalar2=0.25, op0=ALU.mult, op1=ALU.add
                     )
 
-                for i in range(NB):
-                    p1a(1, i)
-                    if i > 0:
-                        evac_a(1, i - 1)
-                    if i % 4 != 3:
-                        tick(i % 2)
-                    for f in range(4 * i, 4 * i + 4):
-                        tab_column(f)
-                evac_a(1, NB - 1)
-                nc.vector.tensor_copy(out=whole_i[:], in_=turns[:])
-                nc.vector.tensor_copy(out=whole_f[:], in_=whole_i[:])
-                nc.vector.tensor_tensor(out=turns[:], in0=turns[:], in1=whole_f[:], op=ALU.subtract)
-                nc.vector.scalar_tensor_tensor(
-                    out=whole_f[:].rearrange("p b f -> p (b f)"),
-                    in0=turns[:].rearrange("p b f -> p (b f)"),
-                    scalar=0.5,
-                    in1=turns[:].rearrange("p b f -> p (b f)"),
-                    op0=ALU.is_gt,
-                    op1=ALU.subtract,
-                )
-                nc.scalar.activation(out=tab[:], in_=whole_f[:], func=ACT.Sin, scale=-TWO_PI)
+                def tab_reduce(step):
+                    flat = "p b f -> p (b f)"
+                    if step == 0:
+                        nc.vector.tensor_copy(out=whole_i[:], in_=turns[:])
+                    elif step == 1:
+                        nc.vector.tensor_copy(out=whole_f[:], in_=whole_i[:])
+                    elif step == 2:
+                        nc.vector.tensor_tensor(out=turns[:], in0=turns[:], in1=whole_f[:], op=ALU.subtract)
+                    elif step == 3:
+                        nc.vector.scalar_tensor_tensor(
+                            out=whole_f[:].rearrange(flat),
+                            in0=turns[:].rearrange(flat),
+                            scalar=0.5,
+                            in1=turns[:].rearrange(flat),
+                            op0=ALU.is_gt,
+                            op1=ALU.subtract,
+                        )
+                    elif step == 4:
+                        nc.scalar.activation(out=tab[:], in_=whole_f[:], func=ACT.Sin, scale=-TWO_PI)
+
+                for n in (1, 2):
+                    for i in range(NB):
+                        p1a(n, i)
+                        evac_a(n - 1 if i == 0 else n, (i - 1) % NB)
+                        if i % 4 != 3:
+                            tick(i % 2)
+                        if n == 1:
+                            for f in range(4 * i, 4 * i + 4):
+                                tab_column(f)
+                        elif 8 <= i < 13:
+                            tab_reduce(i - 8)
 
             with tc.tile_pool(name="bp", bufs=2) as bp:
 
@@ -290,9 +313,9 @@ def tile_multiheadlatentattention_pa_l_kernel(tc, x, w_dq, q_a_norm, w_uq, out):
                         passes(acc, lc, ls, range(G1), G1 * n, G1)
                         accs[(n, i)] = acc
 
-                def hmake(i):
-                    a4 = accs.pop((PARK, i))
-                    a5 = accs.pop((PARK + 1, i))
+                def h_norm(i):
+                    a4 = accs[(PARK, i)]
+                    a5 = accs[(PARK + 1, i)]
                     square(a4, i, PARK)
                     square(a5, i, PARK + 1)
                     ssum = sm.tile([P, 1], F32, name="ssum", tag="ssum", bufs=3)
@@ -303,6 +326,12 @@ def tile_multiheadlatentattention_pa_l_kernel(tc, x, w_dq, q_a_norm, w_uq, out):
                     )
                     rr = sm.tile([P, 1], F32, name="rr", tag="rr", bufs=3)
                     nc.gpsimd.tensor_tensor(out=rr[:], in0=ms[:], in1=neghalf[:], op=ALU.pow)
+                    rrs[i] = rr
+
+                def h_scale(i):
+                    a4 = accs.pop((PARK, i))
+                    a5 = accs.pop((PARK + 1, i))
+                    rr = rrs.pop(i)
                     hb = bp.tile([P, R], BF16, name="hb", tag="hb", bufs=2, align_bytes=64)
                     cr = crs.pop(i)
                     for k, acc in enumerate((a4, a5)):
@@ -322,11 +351,11 @@ def tile_multiheadlatentattention_pa_l_kernel(tc, x, w_dq, q_a_norm, w_uq, out):
                         out=hb[:, 0:1024], in0=cr[:, 0:1024], scalar1=rr[:], scalar2=None, op0=ALU.mult
                     )
                     hbs[i] = hb
+                    cr_load(i + 2)
 
-                def hfin(i):
+                def h_tr(i):
                     hw = hbs.pop(i)[:].bitcast(F32)
-                    hg = bp.tile([P, R], BF16, name="hg", tag="hg", bufs=1, align_bytes=64)
-                    hgw = hg[:].bitcast(F32)
+                    bks = []
                     for b in range(3):
                         bk = bank()
                         for jj in range(4):
@@ -336,10 +365,22 @@ def tile_multiheadlatentattention_pa_l_kernel(tc, x, w_dq, q_a_norm, w_uq, out):
                                 in_=hw[:, 128 * j : 128 * (j + 1)],
                                 identity=ident[:],
                             )
+                        bks.append(bk)
+                    xbank[i] = bks
+
+                def h_out(i):
+                    hg = bp.tile([P, R], BF16, name="hg", tag="hg", bufs=1, align_bytes=64)
+                    hgw = hg[:].bitcast(F32)
+                    bks = xbank.pop(i)
+                    for b in range(3):
                         nc.scalar.copy(
                             out=hgw[:, 512 * b : 512 * (b + 1)].rearrange("p (g r u) -> p g r u", g=2, u=2),
-                            in_=bk[:].rearrange("p (g u r) -> p g r u", g=2, u=2),
+                            in_=bks[b][:].rearrange("p (g u r) -> p g r u", g=2, u=2),
                         )
+                    xgrp[i] = hg
+
+                def h_qnt(i):
+                    hg = xgrp.pop(i)
                     c = xp.tile([P, 768], U32, name="hc", tag="xc", bufs=NB, align_bytes=64)
                     s = xp.tile([P, 768], U8, name="hs", tag="xs", bufs=NB, align_bytes=64)
                     nc.vector.quantize_mx(out=c[:, 0:512].bitcast(FP8X4), scales=s[:, 0:512], in_=hg[:, 0:2048])
@@ -361,53 +402,57 @@ def tile_multiheadlatentattention_pa_l_kernel(tc, x, w_dq, q_a_norm, w_uq, out):
                     cosb = tab[:, b, 64:128].unsqueeze(1).unsqueeze(1).to_broadcast([P, 2, 2, 64])
                     sinb = tab[:, b, 0:64].unsqueeze(1).unsqueeze(1).to_broadcast([P, 2, 2, 64])
                     rot = av[:, :, 128:256].rearrange("q h (s f) -> q h s f", s=2)
-                    ra = sp.tile([P, 2, 2, 64], F32, name="ra", tag="ra", bufs=2)
-                    rb = sp.tile([P, 2, 2, 64], F32, name="rb", tag="rb", bufs=2)
+                    ra = sp.tile([P, 2, 2, 64], F32, name="ra", tag="ra", bufs=3)
+                    rb = sp.tile([P, 2, 2, 64], F32, name="rb", tag="rb", bufs=3)
                     nc.vector.tensor_tensor(out=ra[:], in0=rot, in1=cosb, op=ALU.mult)
                     nc.vector.tensor_tensor(out=rb[:], in0=rot, in1=sinb, op=ALU.mult)
                     nc.scalar.copy(out=sv[:, :, 0:128], in_=av[:, :, 0:128])
-                    nc.vector.tensor_tensor(out=sv[:, :, 128:192], in0=ra[:, :, 0, :], in1=rb[:, :, 1, :], op=ALU.subtract)
-                    nc.vector.tensor_tensor(out=sv[:, :, 192:256], in0=ra[:, :, 1, :], in1=rb[:, :, 0, :], op=ALU.add)
+                    nc.gpsimd.tensor_tensor(out=sv[:, :, 128:192], in0=ra[:, :, 0, :], in1=rb[:, :, 1, :], op=ALU.subtract)
+                    nc.gpsimd.tensor_tensor(out=sv[:, :, 192:256], in0=ra[:, :, 1, :], in1=rb[:, :, 0, :], op=ALU.add)
                     nc.sync.dma_start(out=o2[128 * i : 128 * (i + 1), 512 * m : 512 * (m + 1)], in_=st[:])
 
-                for n in (2, 3):
-                    for i in range(NB):
-                        p1a(n, i)
-                        if i > 0:
-                            evac_a(n, i - 1)
-                        if n == 2:
-                            if i % 4 != 3:
-                                tick(i % 2)
-                        elif i < 8:
-                            tick(i % 2)
-                        elif i == 8:
-                            flush()
-                        if n == 3 and i == 6:
-                            cr_load(0)
-                        if n == 3 and i == 12:
-                            cr_load(1)
-                    evac_a(n, NB - 1)
+                for i in range(NB):
+                    p1a(3, i)
+                    evac_a(2 if i == 0 else 3, (i - 1) % NB)
+                    if i < 8:
+                        tick(i % 2)
+                    elif i == 8:
+                        flush()
+                    if i == 6 or i == 12:
+                        cr_load(i // 6 - 1)
+                evac_a(3, NB - 1)
 
                 s2 = [(m, i) for m in range(C2) for i in range(NB)]
-                for i in range(NB + 2):
-                    if i < NB:
-                        p1b(i)
-                    else:
-                        p2(s2[i - NB][0], s2[i - NB][1])
+                for i in range(NB):
                     if i >= 2:
-                        hfin(i - 2)
-                    if 1 <= i <= NB:
-                        hmake(i - 1)
-                        cr_load(i + 1)
-                    if i == NB + 1:
-                        evac2(s2[0][0], s2[0][1])
-                    if i % 2 == 0 and i < NB:
-                        tick(0)
+                        h_tr(i - 2)
+                    p1b(i)
+                    if i >= 1:
+                        h_norm(i - 1)
+                    if i >= 2:
+                        h_out(i - 2)
+                    if i % 2 == 0:
+                        tick((i // 2) % 2)
+                    if i >= 1:
+                        h_scale(i - 1)
+                    if i >= 2:
+                        h_qnt(i - 2)
+                h_tr(NB - 2)
+                p2(0, 0)
+                h_norm(NB - 1)
+                h_out(NB - 2)
+                h_scale(NB - 1)
+                h_qnt(NB - 2)
+                for k in range(1, 4):
+                    p2(s2[k][0], s2[k][1])
+                    evac2(s2[k - 1][0], s2[k - 1][1])
+                h_tr(NB - 1)
+                h_out(NB - 1)
+                h_qnt(NB - 1)
 
-        done = 2
-        for k in range(done, len(s2)):
+        for k in range(4, len(s2)):
             p2(s2[k][0], s2[k][1])
             evac2(s2[k - 1][0], s2[k - 1][1])
             if (k * 9) % 20 < 9:
-                tick(1)
+                tick(1 if (k * 9) % 20 < 6 else 0)
         evac2(s2[-1][0], s2[-1][1])

@@ -131,6 +131,11 @@ def tile_multiheadlatentattention_pa_l_kernel(tc, x, w_dq, q_a_norm, w_uq, out):
         with tc.tile_pool(name="s1", bufs=1) as s1:
             gain = s1.tile([P, R], BF16, name="gain")
 
+            def gain_load(n):
+                nc.sync.dma_start(
+                    out=gain[:, 512 * n : 512 * (n + 1)], in_=q_a_norm[512 * n : 512 * (n + 1)].partition_broadcast(P)
+                )
+
             def sorted_view(ap):
                 return ap.rearrange("q (p u e) -> q u p e", u=2, e=2)
 
@@ -162,7 +167,10 @@ def tile_multiheadlatentattention_pa_l_kernel(tc, x, w_dq, q_a_norm, w_uq, out):
                     if i >= NB:
                         return
                     t = hp.tile([P, D], BF16, name="xraw", tag="xraw", bufs=2)
-                    nc.sync.dma_start(out=t[:], in_=x2[128 * i : 128 * (i + 1), :])
+                    parts = 4 if i == 0 else 1
+                    for c in range(parts):
+                        cols = (D // parts * c, D // parts * (c + 1))
+                        nc.sync.dma_start(out=t[:, cols[0] : cols[1]], in_=x2[128 * i : 128 * (i + 1), cols[0] : cols[1]])
                     xraw[i] = t
 
                 def x_tr(i):
@@ -221,7 +229,7 @@ def tile_multiheadlatentattention_pa_l_kernel(tc, x, w_dq, q_a_norm, w_uq, out):
                     w_load(2 * k + 4)
                     w_load(2 * k + 5)
                     if k == 2:
-                        nc.sync.dma_start(out=gain[:], in_=q_a_norm.partition_broadcast(P))
+                        gain_load(0)
                     x_qnt(k)
                     w_qnt(2 * k)
                     w_qnt(2 * k + 1)
@@ -240,6 +248,8 @@ def tile_multiheadlatentattention_pa_l_kernel(tc, x, w_dq, q_a_norm, w_uq, out):
                     x_out(i + 1, (0, 1, 0, 1))
                     x_tr(i + 2)
                     evac_a(0, i - 4)
+                    if i == 12:
+                        gain_load(1)
                     x_qnt(i + 1)
                     if i % 3 != 0:
                         tick(1)
@@ -291,6 +301,8 @@ def tile_multiheadlatentattention_pa_l_kernel(tc, x, w_dq, q_a_norm, w_uq, out):
                         evac_a(n - 1 if i == 0 else n, (i - 1) % NB)
                         if i % 4 != 3:
                             tick(i % 2)
+                        elif i == 11:
+                            gain_load(n + 1)
                         if n == 1:
                             for f in range(4 * i, 4 * i + 4):
                                 tab_column(f)
@@ -393,7 +405,7 @@ def tile_multiheadlatentattention_pa_l_kernel(tc, x, w_dq, q_a_norm, w_uq, out):
                     passes(acc, lc, ls, range(C1), G1 * C1 + C1 * m, C1)
                     accs[(m, i)] = acc
 
-                def evac2(m, i):
+                def evac2(m, i, sums=nc.gpsimd):
                     acc = accs.pop((m, i))
                     av = acc[:].rearrange("q (h f) -> q h f", h=2)
                     st = sp.tile([P, 512], F32, name="st", tag="st", bufs=4)
@@ -407,8 +419,8 @@ def tile_multiheadlatentattention_pa_l_kernel(tc, x, w_dq, q_a_norm, w_uq, out):
                     nc.vector.tensor_tensor(out=ra[:], in0=rot, in1=cosb, op=ALU.mult)
                     nc.vector.tensor_tensor(out=rb[:], in0=rot, in1=sinb, op=ALU.mult)
                     nc.scalar.copy(out=sv[:, :, 0:128], in_=av[:, :, 0:128])
-                    nc.gpsimd.tensor_tensor(out=sv[:, :, 128:192], in0=ra[:, :, 0, :], in1=rb[:, :, 1, :], op=ALU.subtract)
-                    nc.gpsimd.tensor_tensor(out=sv[:, :, 192:256], in0=ra[:, :, 1, :], in1=rb[:, :, 0, :], op=ALU.add)
+                    sums.tensor_tensor(out=sv[:, :, 128:192], in0=ra[:, :, 0, :], in1=rb[:, :, 1, :], op=ALU.subtract)
+                    sums.tensor_tensor(out=sv[:, :, 192:256], in0=ra[:, :, 1, :], in1=rb[:, :, 0, :], op=ALU.add)
                     nc.sync.dma_start(out=o2[128 * i : 128 * (i + 1), 512 * m : 512 * (m + 1)], in_=st[:])
 
                 for i in range(NB):
@@ -420,6 +432,8 @@ def tile_multiheadlatentattention_pa_l_kernel(tc, x, w_dq, q_a_norm, w_uq, out):
                         flush()
                     if i == 6 or i == 12:
                         cr_load(i // 6 - 1)
+                    if i == 9 or i == 10:
+                        gain_load(i - 5)
                 evac_a(3, NB - 1)
 
                 s2 = [(m, i) for m in range(C2) for i in range(NB)]
@@ -455,4 +469,4 @@ def tile_multiheadlatentattention_pa_l_kernel(tc, x, w_dq, q_a_norm, w_uq, out):
             evac2(s2[k - 1][0], s2[k - 1][1])
             if (k * 9) % 20 < 9:
                 tick(1 if (k * 9) % 20 < 6 else 0)
-        evac2(s2[-1][0], s2[-1][1])
+        evac2(s2[-1][0], s2[-1][1], nc.vector)

from contextlib import ExitStack

import concourse.mybir as mybir
from concourse.masks import make_identity

F32 = mybir.dt.float32
BF16 = mybir.dt.bfloat16
U32 = mybir.dt.uint32
U8 = mybir.dt.uint8
I32 = mybir.dt.int32
FP8X4 = mybir.dt.float8_e4m3fn_x4
ALU = mybir.AluOpType
ACT = mybir.ActivationFunctionType
AX = mybir.AxisListType

P = 128
TOK = 2048
NB = TOK // P
D = 4096
G1 = D // 512
R = 3072
C1 = R // 512
FO = 4096
C2 = FO // 512
PARK = 4
EPS = 1e-6
TWO_PI = 6.283185307179586
FLOPS = 2 * TOK * D * R + 2 * TOK * R * FO

WSLOTS = 24


def tile_multiheadlatentattention_pa_l_kernel(tc, x, w_dq, q_a_norm, w_uq, out):
    nc = tc.nc
    x2 = x.rearrange("b s d -> (b s) d")
    o2 = out.rearrange("b s h f -> (b s) (h f)")

    wlist = [(0, n, g) for n in range(C1) for g in range(G1)] + [(1, m, g) for m in range(C2) for g in range(C1)]
    NW = len(wlist)
    raw = {}
    grp = {}
    codes = {}
    xraw = {}
    xgrp = {}
    xbank = {}
    xcod = {}
    hcod = {}
    accs = {}
    crs = {}
    rrs = {}
    hbs = {}

    with ExitStack() as ctx:
        keep = ctx.enter_context(tc.tile_pool(name="keep", bufs=1))
        xp = ctx.enter_context(tc.tile_pool(name="xp", bufs=NB))
        wp = ctx.enter_context(tc.tile_pool(name="wp", bufs=4))
        sp = ctx.enter_context(tc.tile_pool(name="sp", bufs=4))
        sm = ctx.enter_context(tc.tile_pool(name="sm", bufs=3))
        ps = ctx.enter_context(tc.psum_pool(name="ps", bufs=8))
        ctx.enter_context(tc.manual_schedule())

        ident = keep.tile([P, P], F32, name="ident")
        make_identity(nc, ident[:])
        neghalf = keep.tile([P, 1], F32, name="neghalf")
        nc.vector.memset(neghalf[:], -0.5)
        ss = keep.tile([P, NB, 8], F32, name="ss")
        tab = keep.tile([P, 8, 128], F32, name="tab")

        def w_load(q):
            if q >= NW:
                return
            kind, n, g = wlist[q]
            src = w_dq if kind == 0 else w_uq
            t = wp.tile([P, 4, 512], BF16, name="wraw", tag="wraw", bufs=4)
            nc.sync.dma_start(
                out=t[:],
                in_=src[512 * g : 512 * (g + 1), 512 * n : 512 * (n + 1)].rearrange("(p j) c -> p j c", j=4),
            )
            raw[q] = t

        def w_ilv(q, eng):
            t = wp.tile([P, 2048], BF16, name="wgrp", tag="wgrp", bufs=3, align_bytes=64)
            o = t[:].rearrange("p (c j) -> p c j", j=4)
            i = raw.pop(q)[:].rearrange("p j c -> p c j")
            if eng == 0:
                nc.vector.tensor_copy(out=o, in_=i)
            else:
                nc.scalar.copy(out=o, in_=i)
            grp[q] = t

        def w_qnt(q):
            c = wp.tile([P, 512], U32, name="wc", tag="wc", bufs=WSLOTS, align_bytes=64)
            s = wp.tile([P, 512], U8, name="ws", tag="ws", bufs=WSLOTS, align_bytes=64)
            nc.vector.quantize_mx(out=c[:].bitcast(FP8X4), scales=s[:], in_=grp.pop(q)[:])
            codes[q] = (c, s)

        tick_state = [8, 8]

        def tick(eng):
            q = tick_state[0]
            if q < NW:
                w_ilv(q, eng)
                w_load(q + 4)
                tick_state[0] = q + 1
            while tick_state[1] < tick_state[0] - (1 if tick_state[0] < NW else 0):
                w_qnt(tick_state[1])
                tick_state[1] = tick_state[1] + 1

        def flush():
            while tick_state[1] < tick_state[0]:
                w_qnt(tick_state[1])
                tick_state[1] = tick_state[1] + 1

        def passes(acc, lc, ls, glist, qbase, ng):
            for g in glist:
                c, s = codes[qbase + g]
                nc.tensor.matmul_mx(
                    out=acc[:],
                    lhsT=lc[:, 128 * g : 128 * (g + 1)].bitcast(FP8X4),
                    lhsT_scale=ls[:, 128 * g : 128 * (g + 1)],
                    rhs=c[:].bitcast(FP8X4),
                    rhs_scale=s[:],
                    start=(g == 0),
                    stop=(g == ng - 1),
                )

        def bank():
            b = ps.tile([P, 512], F32, name="bank", tag="bank", bufs=8)
            return b

        with tc.tile_pool(name="s1", bufs=1) as s1:
            gain = s1.tile([P, R], BF16, name="gain")

            def gain_load(n):
                nc.sync.dma_start(
                    out=gain[:, 512 * n : 512 * (n + 1)], in_=q_a_norm[512 * n : 512 * (n + 1)].partition_broadcast(P)
                )

            def sorted_view(ap):
                return ap.rearrange("q (p u e) -> q u p e", u=2, e=2)

            def square(acc, i, n):
                jk = s1.tile([P, 512], BF16, name="junk", tag="junk", bufs=2)
                nc.scalar.activation(out=jk[:], in_=acc[:], func=ACT.Square, accum_out=ss[:, i, n : n + 1])

            def evac_a(n, i):
                acc = accs.pop((n, i))
                square(acc, i, n)
                st = sp.tile([P, 512], F32, name="st", tag="st", bufs=4)
                nc.vector.tensor_tensor(
                    out=st[:].rearrange("q (u p e) -> q u p e", u=2, e=2),
                    in0=sorted_view(acc[:]),
                    in1=sorted_view(gain[:, 512 * n : 512 * (n + 1)]),
                    op=ALU.mult,
                )
                nc.sync.dma_start(out=o2[128 * i : 128 * (i + 1), 512 * n : 512 * (n + 1)], in_=st[:])

            def p1a(n, i):
                acc = bank()
                lc, ls = xcod[i]
                passes(acc, lc, ls, range(G1), G1 * n, G1)
                accs[(n, i)] = acc

            with tc.tile_pool(name="hp", bufs=2) as hp:

                def x_load(i):
                    if i >= NB:
                        return
                    t = hp.tile([P, D], BF16, name="xraw", tag="xraw", bufs=2)
                    parts = 4 if i == 0 else 1
                    for c in range(parts):
                        cols = (D // parts * c, D // parts * (c + 1))
                        nc.sync.dma_start(out=t[:, cols[0] : cols[1]], in_=x2[128 * i : 128 * (i + 1), cols[0] : cols[1]])
                    xraw[i] = t

                def x_tr(i):
                    if i >= NB:
                        return
                    xw = xraw.pop(i)[:].bitcast(F32)
                    bks = []
                    for b in range(4):
                        bk = bank()
                        for jj in range(4):
                            g = 2 * b + jj // 2
                            u = jj % 2
                            nc.tensor.transpose(
                                out=bk[:, 128 * jj : 128 * (jj + 1)],
                                in_=xw[:, 256 * g + u : 256 * (g + 1) : 2],
                                identity=ident[:],
                            )
                        bks.append(bk)
                    xbank[i] = bks
                    x_load(i + 2)

                def x_out(i, engs):
                    if i >= NB:
                        return
                    xg = hp.tile([P, D], BF16, name="xgrp", tag="xgrp", bufs=2, align_bytes=64)
                    xgw = xg[:].bitcast(F32)
                    bks = xbank.pop(i)
                    for b in range(4):
                        o = xgw[:, 512 * b : 512 * (b + 1)].rearrange("p (g r u) -> p g r u", g=2, u=2)
                        i_ = bks[b][:].rearrange("p (g u r) -> p g r u", g=2, u=2)
                        if engs[b] == 0:
                            nc.vector.tensor_copy(out=o, in_=i_)
                        else:
                            nc.scalar.copy(out=o, in_=i_)
                    xgrp[i] = xg

                def x_qnt(i):
                    if i >= NB:
                        return
                    c = xp.tile([P, 1024], U32, name="xc", tag="xc", bufs=NB, align_bytes=64)
                    s = xp.tile([P, 1024], U8, name="xs", tag="xs", bufs=NB, align_bytes=64)
                    nc.vector.quantize_mx(out=c[:].bitcast(FP8X4), scales=s[:], in_=xgrp.pop(i)[:])
                    xcod[i] = (c, s)

                x_load(0)
                w_load(0)
                w_load(1)
                x_load(1)
                w_load(2)
                w_load(3)
                x_tr(0)
                for k in range(4):
                    x_out(k, (0, 1, 0, 1))
                    w_ilv(2 * k, 0)
                    w_ilv(2 * k + 1, 1)
                    w_load(2 * k + 4)
                    w_load(2 * k + 5)
                    if k == 2:
                        gain_load(0)
                    x_qnt(k)
                    w_qnt(2 * k)
                    w_qnt(2 * k + 1)
                    accs[(0, k)] = bank()
                    lc, ls = xcod[k]
                    passes(accs[(0, k)], lc, ls, range(2 * k), 0, G1)
                    x_tr(k + 1)
                    for kk in range(k + 1):
                        lc, ls = xcod[kk]
                        passes(accs[(0, kk)], lc, ls, (2 * k, 2 * k + 1), 0, G1)
                x_out(4, (0, 1, 0, 1))
                x_tr(5)
                x_qnt(4)
                for i in range(4, NB):
                    p1a(0, i)
                    x_out(i + 1, (0, 1, 0, 1))
                    x_tr(i + 2)
                    evac_a(0, i - 4)
                    if i == 12:
                        gain_load(1)
                    x_qnt(i + 1)
                    if i % 3 != 0:
                        tick(1)
                for i in range(NB - 4, NB - 1):
                    evac_a(0, i)
                flush()

            with tc.tile_pool(name="tb", bufs=1) as tb:
                posi = tb.tile([P, 8], I32, name="posi")
                nc.gpsimd.iota(posi[:], pattern=[[128, 8]], base=0, channel_multiplier=1)
                posf = tb.tile([P, 8], F32, name="posf")
                nc.vector.tensor_copy(out=posf[:], in_=posi[:])
                turns = tb.tile([P, 8, 128], F32, name="turns")
                whole_i = tb.tile([P, 8, 128], I32, name="whole_i")
                whole_f = tb.tile([P, 8, 128], F32, name="whole_f")

                def tab_column(f):
                    inv = (10000.0 ** (-f / 64.0)) / TWO_PI
                    nc.gpsimd.tensor_scalar(
                        out=turns[:, :, f], in0=posf[:], scalar1=inv, scalar2=0.0, op0=ALU.mult, op1=ALU.add
                    )
                    nc.gpsimd.tensor_scalar(
                        out=turns[:, :, 64 + f], in0=posf[:], scalar1=inv, scalar2=0.25, op0=ALU.mult, op1=ALU.add
                    )

                def tab_reduce(step):
                    flat = "p b f -> p (b f)"
                    if step == 0:
                        nc.vector.tensor_copy(out=whole_i[:], in_=turns[:])
                    elif step == 1:
                        nc.vector.tensor_copy(out=whole_f[:], in_=whole_i[:])
                    elif step == 2:
                        nc.vector.tensor_tensor(out=turns[:], in0=turns[:], in1=whole_f[:], op=ALU.subtract)
                    elif step == 3:
                        nc.vector.scalar_tensor_tensor(
                            out=whole_f[:].rearrange(flat),
                            in0=turns[:].rearrange(flat),
                            scalar=0.5,
                            in1=turns[:].rearrange(flat),
                            op0=ALU.is_gt,
                            op1=ALU.subtract,
                        )
                    elif step == 4:
                        nc.scalar.activation(out=tab[:], in_=whole_f[:], func=ACT.Sin, scale=-TWO_PI)

                for n in (1, 2):
                    for i in range(NB):
                        p1a(n, i)
                        evac_a(n - 1 if i == 0 else n, (i - 1) % NB)
                        if i % 4 != 3:
                            tick(i % 2)
                        elif i == 11:
                            gain_load(n + 1)
                        if n == 1:
                            for f in range(4 * i, 4 * i + 4):
                                tab_column(f)
                        elif 8 <= i < 13:
                            tab_reduce(i - 8)

            with tc.tile_pool(name="bp", bufs=2) as bp:

                def cr_load(i):
                    if i >= NB:
                        return
                    t = bp.tile([P, 512 * PARK], F32, name="cr", tag="cr", bufs=2)
                    nc.sync.dma_start(out=t[:], in_=o2[128 * i : 128 * (i + 1), 0 : 512 * PARK])
                    crs[i] = t

                def p1b(i):
                    lc, ls = xcod.pop(i)
                    for n in (PARK, PARK + 1):
                        acc = bank()
                        passes(acc, lc, ls, range(G1), G1 * n, G1)
                        accs[(n, i)] = acc

                def h_norm(i):
                    a4 = accs[(PARK, i)]
                    a5 = accs[(PARK + 1, i)]
                    square(a4, i, PARK)
                    square(a5, i, PARK + 1)
                    ssum = sm.tile([P, 1], F32, name="ssum", tag="ssum", bufs=3)
                    nc.vector.tensor_reduce(out=ssum[:], in_=ss[:, i, 0:C1], axis=AX.X, op=ALU.add)
                    ms = sm.tile([P, 1], F32, name="ms", tag="ms", bufs=3)
                    nc.vector.tensor_scalar(
                        out=ms[:], in0=ssum[:], scalar1=1.0 / R, scalar2=EPS, op0=ALU.mult, op1=ALU.add
                    )
                    rr = sm.tile([P, 1], F32, name="rr", tag="rr", bufs=3)
                    nc.gpsimd.tensor_tensor(out=rr[:], in0=ms[:], in1=neghalf[:], op=ALU.pow)
                    rrs[i] = rr

                def h_scale(i):
                    a4 = accs.pop((PARK, i))
                    a5 = accs.pop((PARK + 1, i))
                    rr = rrs.pop(i)
                    hb = bp.tile([P, R], BF16, name="hb", tag="hb", bufs=2, align_bytes=64)
                    cr = crs.pop(i)
                    for k, acc in enumerate((a4, a5)):
                        n = PARK + k
                        for u in range(2):
                            lo = 512 * n + 256 * u
                            nc.vector.scalar_tensor_tensor(
                                out=hb[:, lo : lo + 256].rearrange("q (p e) -> q p e", e=2),
                                in0=sorted_view(acc[:])[:, u],
                                scalar=rr[:],
                                in1=sorted_view(gain[:, 512 * n : 512 * (n + 1)])[:, u],
                                op0=ALU.mult,
                                op1=ALU.mult,
                            )
                    nc.scalar.activation(out=hb[:, 1024:2048], in_=cr[:, 1024:2048], func=ACT.Copy, scale=rr[:])
                    nc.vector.tensor_scalar(
                        out=hb[:, 0:1024], in0=cr[:, 0:1024], scalar1=rr[:], scalar2=None, op0=ALU.mult
                    )
                    hbs[i] = hb
                    cr_load(i + 2)

                def h_tr(i):
                    hw = hbs.pop(i)[:].bitcast(F32)
                    bks = []
                    for b in range(3):
                        bk = bank()
                        for jj in range(4):
                            j = 4 * b + jj
                            nc.tensor.transpose(
                                out=bk[:, 128 * jj : 128 * (jj + 1)],
                                in_=hw[:, 128 * j : 128 * (j + 1)],
                                identity=ident[:],
                            )
                        bks.append(bk)
                    xbank[i] = bks

                def h_out(i):
                    hg = bp.tile([P, R], BF16, name="hg", tag="hg", bufs=1, align_bytes=64)
                    hgw = hg[:].bitcast(F32)
                    bks = xbank.pop(i)
                    for b in range(3):
                        nc.scalar.copy(
                            out=hgw[:, 512 * b : 512 * (b + 1)].rearrange("p (g r u) -> p g r u", g=2, u=2),
                            in_=bks[b][:].rearrange("p (g u r) -> p g r u", g=2, u=2),
                        )
                    xgrp[i] = hg

                def h_qnt(i):
                    hg = xgrp.pop(i)
                    c = xp.tile([P, 768], U32, name="hc", tag="xc", bufs=NB, align_bytes=64)
                    s = xp.tile([P, 768], U8, name="hs", tag="xs", bufs=NB, align_bytes=64)
                    nc.vector.quantize_mx(out=c[:, 0:512].bitcast(FP8X4), scales=s[:, 0:512], in_=hg[:, 0:2048])
                    nc.vector.quantize_mx(out=c[:, 512:768].bitcast(FP8X4), scales=s[:, 512:768], in_=hg[:, 2048:3072])
                    hcod[i] = (c, s)

                def p2(m, i):
                    acc = bank()
                    lc, ls = hcod[i]
                    passes(acc, lc, ls, range(C1), G1 * C1 + C1 * m, C1)
                    accs[(m, i)] = acc

                def evac2(m, i, sums=nc.gpsimd):
                    acc = accs.pop((m, i))
                    av = acc[:].rearrange("q (h f) -> q h f", h=2)
                    st = sp.tile([P, 512], F32, name="st", tag="st", bufs=4)
                    sv = st[:].rearrange("q (h f) -> q h f", h=2)
                    b = i % 8
                    cosb = tab[:, b, 64:128].unsqueeze(1).unsqueeze(1).to_broadcast([P, 2, 2, 64])
                    sinb = tab[:, b, 0:64].unsqueeze(1).unsqueeze(1).to_broadcast([P, 2, 2, 64])
                    rot = av[:, :, 128:256].rearrange("q h (s f) -> q h s f", s=2)
                    ra = sp.tile([P, 2, 2, 64], F32, name="ra", tag="ra", bufs=3)
                    rb = sp.tile([P, 2, 2, 64], F32, name="rb", tag="rb", bufs=3)
                    nc.vector.tensor_tensor(out=ra[:], in0=rot, in1=cosb, op=ALU.mult)
                    nc.vector.tensor_tensor(out=rb[:], in0=rot, in1=sinb, op=ALU.mult)
                    nc.scalar.copy(out=sv[:, :, 0:128], in_=av[:, :, 0:128])
                    sums.tensor_tensor(out=sv[:, :, 128:192], in0=ra[:, :, 0, :], in1=rb[:, :, 1, :], op=ALU.subtract)
                    sums.tensor_tensor(out=sv[:, :, 192:256], in0=ra[:, :, 1, :], in1=rb[:, :, 0, :], op=ALU.add)
                    nc.sync.dma_start(out=o2[128 * i : 128 * (i + 1), 512 * m : 512 * (m + 1)], in_=st[:])

                for i in range(NB):
                    p1a(3, i)
                    evac_a(2 if i == 0 else 3, (i - 1) % NB)
                    if i < 8:
                        tick(i % 2)
                    elif i == 8:
                        flush()
                    if i == 6 or i == 12:
                        cr_load(i // 6 - 1)
                    if i == 9 or i == 10:
                        gain_load(i - 5)
                evac_a(3, NB - 1)

                s2 = [(m, i) for m in range(C2) for i in range(NB)]
                for i in range(NB):
                    if i >= 2:
                        h_tr(i - 2)
                    p1b(i)
                    if i >= 1:
                        h_norm(i - 1)
                    if i >= 2:
                        h_out(i - 2)
                    if i % 2 == 0:
                        tick((i // 2) % 2)
                    if i >= 1:
                        h_scale(i - 1)
                    if i >= 2:
                        h_qnt(i - 2)
                h_tr(NB - 2)
                p2(0, 0)
                h_norm(NB - 1)
                h_out(NB - 2)
                h_scale(NB - 1)
                h_qnt(NB - 2)
                for k in range(1, 4):
                    p2(s2[k][0], s2[k][1])
                    evac2(s2[k - 1][0], s2[k - 1][1])
                h_tr(NB - 1)
                h_out(NB - 1)
                h_qnt(NB - 1)

        for k in range(4, len(s2)):
            p2(s2[k][0], s2[k][1])
            evac2(s2[k - 1][0], s2[k - 1][1])
            if (k * 9) % 20 < 9:
                tick(1 if (k * 9) % 20 < 6 else 0)
        evac2(s2[-1][0], s2[-1][1], nc.vector)
